import numpy as np
import ml_dtypes


def mxq(x, axis, fmt="e4m3"):
    dtype, down = {"e4m3": (ml_dtypes.float8_e4m3fn, 7), "e5m2": (ml_dtypes.float8_e5m2, 14)}[fmt]
    v = np.moveaxis(np.asarray(x, np.float32).astype(ml_dtypes.bfloat16).astype(np.float64), axis, -1)
    blocks = v.reshape(v.shape[:-1] + (-1, 32))
    amax = np.abs(blocks).max(-1, keepdims=True)
    byte = np.maximum(np.where(amax > 0, np.frexp(amax)[1] - 1 + 127, 0) - down, 1)
    scale = np.exp2(byte - 127.0)
    codes = (blocks / scale).astype(np.float32).astype(dtype).astype(np.float64)
    return np.moveaxis((codes * scale).reshape(v.shape), -1, axis)


WIDE = False


def mx_kscale(k):
    if not WIDE:
        return np.ones(k)
    levels = np.array([20, -20, 10, -10, 0])
    a = np.random.permutation(np.resize(levels, k // 512 * 4)).reshape(k // 512, 4)
    idx = np.arange(k)
    return np.exp2(a[idx // 512, idx % 128 // 32])


BF16 = ml_dtypes.bfloat16


def bf(x):
    return np.asarray(x, np.float32).astype(BF16)


def f64(x):
    return np.asarray(x).astype(np.float64)


B, H, L, D = 8, 2, 512, 512
NEG = -100.0


def unskew(g):
    g = g.reshape(B * H, L, L)
    keep = np.tril(np.ones((L, L), dtype=bool))
    g = np.where(keep[None, :, :], g, 0.0)
    g = np.pad(g, ((0, 0), (1, 0), (0, 0)))
    g = g.reshape(B * H, L, L + 1)[:, :, 1:]
    return g.reshape(B, H, L, L)


def setup_inputs():
    s = mx_kscale(L)
    i = np.arange(L)[:, None]
    j = np.arange(L)[None, :]
    m = L - 1 - i + j
    sg = np.where(m < L, s[np.minimum(m, L - 1)], 1.0)
    q = np.random.standard_normal((B, H, L, D))
    e = np.random.standard_normal((H, L, D)) / np.sqrt(D) / s[None, :, None]
    g = np.random.standard_normal((B, H, L, L)) * np.exp2(np.random.randint(-12, 1, (B, H, L, 1))) * 8.0 * sg
    return {"q": bf(q), "e": bf(e), "grad_out": bf(g)}


def reference(q, e, grad_out):
    grel = unskew(f64(grad_out))
    return mxq(grel, 3, "e5m2") @ mxq(f64(e), 1, "e4m3")

@@ -1,0 +1,184 @@
+from contextlib import ExitStack
+
+import concourse.mybir as mybir
+from concourse.masks import make_identity
+
+BF16 = mybir.dt.bfloat16
+F32 = mybir.dt.float32
+I32 = mybir.dt.int32
+U32 = mybir.dt.uint32
+U8 = mybir.dt.uint8
+E4X4 = mybir.dt.float8_e4m3fn_x4
+E5X4 = mybir.dt.float8_e5m2_x4
+ALU = mybir.AluOpType
+
+P = 128
+NB = 16
+L = 512
+LL = L * L
+SKEW = L + 1
+
+FLOPS = 2 * NB * L * L * L
+BYTES = NB * L * L * 4 + 2 * L * L * 2 + NB * (L * (L + 1) // 2) * 2
+
+TILE_COLS = (256, 256, 512, 512)
+LOAD_AT = (128, 0, 128, 0)
+GROUPS = ((15, 1), (14, 1), (12, 2), (8, 4), (4, 4), (0, 4))
+
+
+def tile_subsampledrelativeattention_t_kernel(tc, q, e, grad_out, out):
+    nc = tc.nc
+    flat = grad_out.rearrange("b h i j -> (b h i j)")
+    mats = grad_out.rearrange("b h i j -> (b h) (i j)")
+
+    def skewed(b0, count, t):
+        width = P * (t + 1)
+        if t == 0:
+            start = b0 * LL - P
+            src = flat[start : start + count * LL].rearrange("(g x) -> g x", x=LL)
+            first = 0
+        else:
+            src = mats[b0 : b0 + count, :]
+            first = 65536 * t - P
+        rows = src[:, first : first + P * SKEW].rearrange("g (i c) -> i g c", c=SKEW)
+        return rows[:, :, 1 : 1 + width]
+
+    with ExitStack() as ctx:
+        const = ctx.enter_context(tc.tile_pool(name="const", bufs=1))
+        gpool = ctx.enter_context(tc.tile_pool(name="gpool", bufs=1))
+        work = ctx.enter_context(tc.tile_pool(name="work", bufs=3))
+        opool = ctx.enter_context(tc.tile_pool(name="opool", bufs=6))
+        pst = ctx.enter_context(tc.psum_pool(name="pst", bufs=2))
+        pso = ctx.enter_context(tc.psum_pool(name="pso", bufs=4))
+
+        ident = const.tile([P, P], F32, name="ident")
+        make_identity(nc, ident[:])
+        zero = const.tile([P, P], F32, name="zero")
+        nc.vector.memset(zero[:], 0.0)
+        idx = const.tile([P, 64], I32, name="idx")
+        nc.gpsimd.iota(idx[:], pattern=[[2, 64]], base=0, channel_multiplier=1)
+        keep_lo = const.tile([P, 64], I32, name="keep_lo")
+        keep_hi = const.tile([P, 64], I32, name="keep_hi")
+        keep_hs = const.tile([P, 64], I32, name="keep_hs")
+        mask = const.tile([P, 64], I32, name="mask")
+        nc.vector.tensor_scalar(
+            out=keep_lo[:], in0=idx[:], scalar1=127.0, scalar2=65535.0, op0=ALU.is_ge, op1=ALU.mult
+        )
+        nc.vector.tensor_scalar(
+            out=keep_hi[:], in0=idx[:], scalar1=126.0, scalar2=65535.0, op0=ALU.is_ge, op1=ALU.mult
+        )
+        nc.vector.tensor_single_scalar(out=keep_hs[:], in_=keep_hi[:], scalar=16, op=ALU.logical_shift_left)
+        nc.vector.tensor_tensor(out=mask[:], in0=keep_lo[:], in1=keep_hs[:], op=ALU.bitwise_or)
+
+        e_raw = [None, None]
+        g_tiles = {}
+
+        def load_e(h):
+            raw = const.tile([P, 4 * L], BF16, name="e_raw%d" % h)
+            nc.sync.dma_start(
+                out=raw[:].rearrange("p (u x) -> p u x", u=2),
+                in_=e[h].rearrange("(u p k) d -> p u (k d)", u=2, p=P, k=2),
+            )
+            e_raw[h] = raw
+
+        def load_group(gi):
+            b0, count = GROUPS[gi]
+            for t in (3, 2, 1, 0):
+                gt = gpool.tile([P, count * TILE_COLS[t]], BF16, name="g%d_%d" % (gi, t))
+                words = gt[:].bitcast(I32).rearrange("p (g w) -> p g w", g=count)
+                cols = gt[:].rearrange("p (g w) -> p g w", g=count)
+                lo = LOAD_AT[t]
+                width = P * (t + 1)
+                if lo:
+                    nc.vector.memset(words[:, :, 0 : lo // 2], 0)
+                if t == 0 and b0 == 0:
+                    nc.vector.memset(gt[0:1, lo : lo + P], 0.0)
+                    nc.sync.dma_start(
+                        out=cols[:, 1:count, lo : lo + width], in_=skewed(1, count - 1, 0)
+                    )
+                    for r0, r1 in ((16, P), (1, 16)):
+                        first = SKEW * r0 - P
+                        nc.sync.dma_start(
+                            out=gt[r0:r1, lo : lo + P],
+                            in_=flat[first : first + (r1 - r0) * SKEW].rearrange("(i c) -> i c", c=SKEW)[:, 1 : 1 + P],
+                        )
+                    nc.sync.dma_start(
+                        out=gt[0:1, lo + P - 1 : lo + P], in_=flat[0:1].rearrange("(a b) -> a b", a=1)
+                    )
+                else:
+                    nc.sync.dma_start(out=cols[:, :, lo : lo + width], in_=skewed(b0, count, t))
+                g_tiles[(gi, t)] = gt
+
+        load_e(1)
+        load_group(0)
+        load_e(0)
+        for gi in range(1, len(GROUPS)):
+            load_group(gi)
+
+        e_codes = const.tile([P, 2 * L], U32, name="e_codes", align_bytes=64)
+        e_scales = const.tile([P, 2 * L], U8, name="e_scales", align_bytes=64)
+        for h in (1, 0):
+            e_grp = const.tile([P, 4 * L], BF16, name="e_grp%d" % h, align_bytes=64)
+            nc.vector.tensor_copy(
+                out=e_grp[:].rearrange("p (d t) -> p d t", t=4),
+                in_=e_raw[h][:].rearrange("p (t d) -> p d t", t=4),
+            )
+            nc.vector.quantize_mx(
+                out=e_codes[:, h * L : (h + 1) * L].bitcast(E4X4),
+                scales=e_scales[:, h * L : (h + 1) * L],
+                in_=e_grp[:],
+            )
+
+        for gi in range(len(GROUPS)):
+            b0, count = GROUPS[gi]
+            for t in range(4):
+                words = g_tiles[(gi, t)][:].bitcast(I32).rearrange("p (g w) -> p g w", g=count)
+                d0 = LOAD_AT[t] // 2
+                nc.vector.tensor_tensor(
+                    out=words[:, :, d0 : d0 + 64],
+                    in0=words[:, :, d0 : d0 + 64],
+                    in1=mask[:].unsqueeze(1).to_broadcast([P, count, 64]),
+                    op=ALU.bitwise_and,
+                )
+            for g in range(count):
+                bh = b0 + g
+                h = bh % 2
+                xa = pst.tile([P, L], F32, name="xa")
+                xb = pst.tile([P, L], F32, name="xb")
+                banks = (xa, xb)
+                for t in range(4):
+                    fw = g_tiles[(gi, t)][:].bitcast(F32).rearrange("p (g w) -> p g w", g=count)
+                    for u in range(2):
+                        if t < 2:
+                            src = zero[:] if u == 0 else fw[:, g, 0:P]
+                        else:
+                            src = fw[:, g, u * P : (u + 1) * P]
+                        at = (t % 2) * 256 + u * P
+                        nc.tensor.transpose(banks[t // 2][:, at : at + P], src, ident[:])
+                grouped = work.tile([P, 4 * L], BF16, name="grouped", align_bytes=64)
+                gw = grouped[:].bitcast(F32).rearrange("p (s b c u) -> p s b c u", s=4, b=4, c=32, u=2)
+                for t in range(4):
+                    at = (t % 2) * 256
+                    nc.vector.tensor_copy(
+                        out=gw[:, :, t, :, :],
+                        in_=banks[t // 2][:, at : at + 256].rearrange("p (u c s) -> p s c u", u=2, c=32, s=4),
+                    )
+                g_codes = work.tile([P, L], U32, name="g_codes", align_bytes=64)
+                g_scales = work.tile([P, L], U8, name="g_scales", align_bytes=64)
+                nc.vector.quantize_mx(out=g_codes[:].bitcast(E5X4), scales=g_scales[:], in_=grouped[:])
+                osb = opool.tile([P, 4 * L], F32, name="osb")
+                for s in range(4):
+                    acc = pso.tile([P, L], F32, name="acc")
+                    nc.tensor.matmul_mx(
+                        out=acc[:],
+                        lhsT=g_codes[:, s * P : (s + 1) * P].bitcast(E5X4),
+                        lhsT_scale=g_scales[:, s * P : (s + 1) * P],
+                        rhs=e_codes[:, h * L : (h + 1) * L].bitcast(E4X4),
+                        rhs_scale=e_scales[:, h * L : (h + 1) * L],
+                        start=True,
+                        stop=True,
+                    )
+                    nc.scalar.copy(out=osb[:, s * L : (s + 1) * L], in_=acc[:])
+                nc.sync.dma_start(
+                    out=out[bh // 2, h].rearrange("(c s) d -> c (s d)", s=4), in_=osb[:]
+                )

@@ -179,6 +179,6 @@ def tile_subsampledrelativeattention_t_kernel(tc, q, e, grad_out, out):
                         stop=True,
                     )
                     nc.scalar.copy(out=osb[:, s * L : (s + 1) * L], in_=acc[:])
-                nc.sync.dma_start(
+                nc.scalar.dma_start(
                     out=out[bh // 2, h].rearrange("(c s) d -> c (s d)", s=4), in_=osb[:]
                 )

@@ -119,9 +119,9 @@ def tile_subsampledrelativeattention_t_kernel(tc, q, e, grad_out, out):
         e_scales = const.tile([P, 2 * L], U8, name="e_scales", align_bytes=64)
         for h in (1, 0):
             e_grp = const.tile([P, 4 * L], BF16, name="e_grp%d" % h, align_bytes=64)
-            nc.vector.tensor_copy(
-                out=e_grp[:].rearrange("p (d t) -> p d t", t=4),
-                in_=e_raw[h][:].rearrange("p (t d) -> p d t", t=4),
+            nc.scalar.copy(
+                out=e_grp[:].rearrange("p (c i t) -> p c t i", i=4, t=4),
+                in_=e_raw[h][:].rearrange("p (t c i) -> p c t i", t=4, i=4),
             )
             nc.vector.quantize_mx(
                 out=e_codes[:, h * L : (h + 1) * L].bitcast(E4X4),
@@ -157,11 +157,10 @@ def tile_subsampledrelativeattention_t_kernel(tc, q, e, grad_out, out):
                         nc.tensor.transpose(banks[t // 2][:, at : at + P], src, ident[:])
                 grouped = work.tile([P, 4 * L], BF16, name="grouped", align_bytes=64)
                 gw = grouped[:].bitcast(F32).rearrange("p (s b c u) -> p s b c u", s=4, b=4, c=32, u=2)
-                for t in range(4):
-                    at = (t % 2) * 256
+                for half in range(2):
                     nc.vector.tensor_copy(
-                        out=gw[:, :, t, :, :],
-                        in_=banks[t // 2][:, at : at + 256].rearrange("p (u c s) -> p s c u", u=2, c=32, s=4),
+                        out=gw[:, :, 2 * half : 2 * half + 2, :, :],
+                        in_=banks[half][:].rearrange("p (b u c s) -> p s b c u", b=2, u=2, c=32, s=4),
                     )
                 g_codes = work.tile([P, L], U32, name="g_codes", align_bytes=64)
                 g_scales = work.tile([P, L], U8, name="g_scales", align_bytes=64)
@@ -178,7 +177,17 @@ def tile_subsampledrelativeattention_t_kernel(tc, q, e, grad_out, out):
                         start=True,
                         stop=True,
                     )
-                    nc.scalar.copy(out=osb[:, s * L : (s + 1) * L], in_=acc[:])
-                nc.scalar.dma_start(
-                    out=out[bh // 2, h].rearrange("(c s) d -> c (s d)", s=4), in_=osb[:]
-                )
+                    last = gi == len(GROUPS) - 1 and g == count - 1
+                    if (last and s % 2 == 1) or (not last and s == 3 and bh % 4 == 1):
+                        nc.vector.tensor_copy(out=osb[:, s * L : (s + 1) * L], in_=acc[:])
+                    else:
+                        nc.scalar.copy(out=osb[:, s * L : (s + 1) * L], in_=acc[:])
+                    if last and s % 2 == 1:
+                        nc.gpsimd.dma_start(
+                            out=out[bh // 2, h].rearrange("(c s) d -> c s d", s=4)[:, s - 1 : s + 1, :],
+                            in_=osb[:, (s - 1) * L : (s + 1) * L].rearrange("p (s d) -> p s d", s=2),
+                        )
+                if not last:
+                    nc.gpsimd.dma_start(
+                        out=out[bh // 2, h].rearrange("(c s) d -> c (s d)", s=4), in_=osb[:]
+                    )

@@ -183,11 +183,11 @@ def tile_subsampledrelativeattention_t_kernel(tc, q, e, grad_out, out):
                     else:
                         nc.scalar.copy(out=osb[:, s * L : (s + 1) * L], in_=acc[:])
                     if last and s % 2 == 1:
-                        nc.gpsimd.dma_start(
+                        nc.sync.dma_start(
                             out=out[bh // 2, h].rearrange("(c s) d -> c s d", s=4)[:, s - 1 : s + 1, :],
                             in_=osb[:, (s - 1) * L : (s + 1) * L].rearrange("p (s d) -> p s d", s=2),
                         )
                 if not last:
-                    nc.gpsimd.dma_start(
+                    nc.sync.dma_start(
                         out=out[bh // 2, h].rearrange("(c s) d -> c (s d)", s=4), in_=osb[:]
                     )

@@ -50,6 +50,7 @@ def tile_subsampledrelativeattention_t_kernel(tc, q, e, grad_out, out):
         opool = ctx.enter_context(tc.tile_pool(name="opool", bufs=6))
         pst = ctx.enter_context(tc.psum_pool(name="pst", bufs=2))
         pso = ctx.enter_context(tc.psum_pool(name="pso", bufs=4))
+        ctx.enter_context(tc.manual_schedule())
 
         ident = const.tile([P, P], F32, name="ident")
         make_identity(nc, ident[:])
@@ -109,29 +110,39 @@ def tile_subsampledrelativeattention_t_kernel(tc, q, e, grad_out, out):
                     nc.sync.dma_start(out=cols[:, :, lo : lo + width], in_=skewed(b0, count, t))
                 g_tiles[(gi, t)] = gt
 
-        load_e(1)
         load_group(0)
+        load_e(1)
+        load_group(1)
         load_e(0)
-        for gi in range(1, len(GROUPS)):
+        for gi in range(2, len(GROUPS)):
             load_group(gi)
 
         e_codes = const.tile([P, 2 * L], U32, name="e_codes", align_bytes=64)
         e_scales = const.tile([P, 2 * L], U8, name="e_scales", align_bytes=64)
-        for h in (1, 0):
-            e_grp = const.tile([P, 4 * L], BF16, name="e_grp%d" % h, align_bytes=64)
+        e_grp = {}
+        seq = [(gi, g) for gi in range(len(GROUPS)) for g in range(GROUPS[gi][1])]
+        n_mats = len(seq)
+        banks = {}
+        grouped = {}
+        codes = {}
+
+        def regroup_e(h):
+            e_grp[h] = const.tile([P, 4 * L], BF16, name="e_grp%d" % h, align_bytes=64)
             nc.scalar.copy(
-                out=e_grp[:].rearrange("p (c i t) -> p c t i", i=4, t=4),
+                out=e_grp[h][:].rearrange("p (c i t) -> p c t i", i=4, t=4),
                 in_=e_raw[h][:].rearrange("p (t c i) -> p c t i", t=4, i=4),
             )
+
+        def quantise_e(h):
             nc.vector.quantize_mx(
                 out=e_codes[:, h * L : (h + 1) * L].bitcast(E4X4),
                 scales=e_scales[:, h * L : (h + 1) * L],
-                in_=e_grp[:],
+                in_=e_grp[h][:],
             )
 
-        for gi in range(len(GROUPS)):
-            b0, count = GROUPS[gi]
-            for t in range(4):
+        def clear_left_of_diagonal(gi):
+            count = GROUPS[gi][1]
+            for t in (3, 2, 1, 0):
                 words = g_tiles[(gi, t)][:].bitcast(I32).rearrange("p (g w) -> p g w", g=count)
                 d0 = LOAD_AT[t] // 2
                 nc.vector.tensor_tensor(
@@ -140,54 +151,95 @@ def tile_subsampledrelativeattention_t_kernel(tc, q, e, grad_out, out):
                     in1=mask[:].unsqueeze(1).to_broadcast([P, count, 64]),
                     op=ALU.bitwise_and,
                 )
-            for g in range(count):
-                bh = b0 + g
-                h = bh % 2
-                xa = pst.tile([P, L], F32, name="xa")
-                xb = pst.tile([P, L], F32, name="xb")
-                banks = (xa, xb)
-                for t in range(4):
-                    fw = g_tiles[(gi, t)][:].bitcast(F32).rearrange("p (g w) -> p g w", g=count)
-                    for u in range(2):
-                        if t < 2:
-                            src = zero[:] if u == 0 else fw[:, g, 0:P]
-                        else:
-                            src = fw[:, g, u * P : (u + 1) * P]
-                        at = (t % 2) * 256 + u * P
-                        nc.tensor.transpose(banks[t // 2][:, at : at + P], src, ident[:])
-                grouped = work.tile([P, 4 * L], BF16, name="grouped", align_bytes=64)
-                gw = grouped[:].bitcast(F32).rearrange("p (s b c u) -> p s b c u", s=4, b=4, c=32, u=2)
-                for half in range(2):
-                    nc.vector.tensor_copy(
-                        out=gw[:, :, 2 * half : 2 * half + 2, :, :],
-                        in_=banks[half][:].rearrange("p (b u c s) -> p s b c u", b=2, u=2, c=32, s=4),
-                    )
-                g_codes = work.tile([P, L], U32, name="g_codes", align_bytes=64)
-                g_scales = work.tile([P, L], U8, name="g_scales", align_bytes=64)
-                nc.vector.quantize_mx(out=g_codes[:].bitcast(E5X4), scales=g_scales[:], in_=grouped[:])
-                osb = opool.tile([P, 4 * L], F32, name="osb")
-                for s in range(4):
-                    acc = pso.tile([P, L], F32, name="acc")
-                    nc.tensor.matmul_mx(
-                        out=acc[:],
-                        lhsT=g_codes[:, s * P : (s + 1) * P].bitcast(E5X4),
-                        lhsT_scale=g_scales[:, s * P : (s + 1) * P],
-                        rhs=e_codes[:, h * L : (h + 1) * L].bitcast(E4X4),
-                        rhs_scale=e_scales[:, h * L : (h + 1) * L],
-                        start=True,
-                        stop=True,
-                    )
-                    last = gi == len(GROUPS) - 1 and g == count - 1
-                    if (last and s % 2 == 1) or (not last and s == 3 and bh % 4 == 1):
-                        nc.vector.tensor_copy(out=osb[:, s * L : (s + 1) * L], in_=acc[:])
+
+        def transposes(n):
+            gi, g = seq[n]
+            count = GROUPS[gi][1]
+            xa = pst.tile([P, L], F32, name="xa")
+            xb = pst.tile([P, L], F32, name="xb")
+            banks[n] = (xa, xb)
+            for t in (3, 2, 1, 0):
+                fw = g_tiles[(gi, t)][:].bitcast(F32).rearrange("p (g w) -> p g w", g=count)
+                for u in range(2):
+                    if t < 2:
+                        src = zero[:] if u == 0 else fw[:, g, 0:P]
                     else:
-                        nc.scalar.copy(out=osb[:, s * L : (s + 1) * L], in_=acc[:])
-                    if last and s % 2 == 1:
-                        nc.sync.dma_start(
-                            out=out[bh // 2, h].rearrange("(c s) d -> c s d", s=4)[:, s - 1 : s + 1, :],
-                            in_=osb[:, (s - 1) * L : (s + 1) * L].rearrange("p (s d) -> p s d", s=2),
-                        )
-                if not last:
+                        src = fw[:, g, u * P : (u + 1) * P]
+                    at = (t % 2) * 256 + u * P
+                    nc.tensor.transpose(banks[n][t // 2][:, at : at + P], src, ident[:])
+
+        def copy_out(n):
+            grp = work.tile([P, 4 * L], BF16, name="grp", align_bytes=64)
+            grouped[n] = grp
+            gw = grp[:].bitcast(F32).rearrange("p (s b c u) -> p s b c u", s=4, b=4, c=32, u=2)
+            for half in (1, 0):
+                nc.vector.tensor_copy(
+                    out=gw[:, :, 2 * half : 2 * half + 2, :, :],
+                    in_=banks[n][half][:].rearrange("p (b u c s) -> p s b c u", b=2, u=2, c=32, s=4),
+                )
+
+        def quantise(n):
+            g_codes = work.tile([P, L], U32, name="g_codes", align_bytes=64)
+            g_scales = work.tile([P, L], U8, name="g_scales", align_bytes=64)
+            codes[n] = (g_codes, g_scales)
+            nc.vector.quantize_mx(out=g_codes[:].bitcast(E5X4), scales=g_scales[:], in_=grouped[n][:])
+
+        def multiply_and_store(n):
+            gi, g = seq[n]
+            bh = GROUPS[gi][0] + g
+            h = bh % 2
+            g_codes, g_scales = codes[n]
+            last = n == n_mats - 1
+            osb = opool.tile([P, 4 * L], F32, name="osb")
+            rows = out[bh // 2, h].rearrange("(c s) d -> c s d", s=4)
+            for s in range(4):
+                acc = pso.tile([P, L], F32, name="acc")
+                nc.tensor.matmul_mx(
+                    out=acc[:],
+                    lhsT=g_codes[:, s * P : (s + 1) * P].bitcast(E5X4),
+                    lhsT_scale=g_scales[:, s * P : (s + 1) * P],
+                    rhs=e_codes[:, h * L : (h + 1) * L].bitcast(E4X4),
+                    rhs_scale=e_scales[:, h * L : (h + 1) * L],
+                    start=True,
+                    stop=True,
+                )
+                if last and s % 2 == 1:
+                    nc.vector.tensor_copy(out=osb[:, s * L : (s + 1) * L], in_=acc[:])
                     nc.sync.dma_start(
-                        out=out[bh // 2, h].rearrange("(c s) d -> c (s d)", s=4), in_=osb[:]
+                        out=rows[:, s - 1 : s + 1, :],
+                        in_=osb[:, (s - 1) * L : (s + 1) * L].rearrange("p (s d) -> p s d", s=2),
                     )
+                else:
+                    nc.scalar.copy(out=osb[:, s * L : (s + 1) * L], in_=acc[:])
+            if not last:
+                nc.sync.dma_start(out=rows, in_=osb[:].rearrange("p (s d) -> p s d", s=4))
+
+        first_of_group = {}
+        at_n = 0
+        for gi in range(len(GROUPS)):
+            first_of_group[at_n] = gi
+            at_n += GROUPS[gi][1]
+
+        regroup_e(1)
+        clear_left_of_diagonal(0)
+        transposes(0)
+        copy_out(0)
+        clear_left_of_diagonal(1)
+        transposes(1)
+        regroup_e(0)
+        for n in range(n_mats):
+            if n == 0:
+                quantise(0)
+                quantise_e(1)
+                copy_out(1)
+                quantise_e(0)
+                clear_left_of_diagonal(2)
+            else:
+                if n + 1 < n_mats:
+                    copy_out(n + 1)
+                quantise(n)
+                if n + 3 in first_of_group:
+                    clear_left_of_diagonal(first_of_group[n + 3])
+            if n + 2 < n_mats:
+                transposes(n + 2)
+            multiply_and_store(n)

@@ -73,6 +73,7 @@ def tile_subsampledrelativeattention_t_kernel(tc, q, e, grad_out, out):
 
         e_raw = [None, None]
         g_tiles = {}
+        corner = const.tile([1, 2], BF16, name="corner")
 
         def load_e(h):
             raw = const.tile([P, 4 * L], BF16, name="e_raw%d" % h)
@@ -103,9 +104,7 @@ def tile_subsampledrelativeattention_t_kernel(tc, q, e, grad_out, out):
                             out=gt[r0:r1, lo : lo + P],
                             in_=flat[first : first + (r1 - r0) * SKEW].rearrange("(i c) -> i c", c=SKEW)[:, 1 : 1 + P],
                         )
-                    nc.sync.dma_start(
-                        out=gt[0:1, lo + P - 1 : lo + P], in_=flat[0:1].rearrange("(a b) -> a b", a=1)
-                    )
+                    nc.sync.dma_start(out=corner[:], in_=flat[0:2].rearrange("(a b) -> a b", a=1))
                 else:
                     nc.sync.dma_start(out=cols[:, :, lo : lo + width], in_=skewed(b0, count, t))
                 g_tiles[(gi, t)] = gt
@@ -142,6 +141,9 @@ def tile_subsampledrelativeattention_t_kernel(tc, q, e, grad_out, out):
 
         def clear_left_of_diagonal(gi):
             count = GROUPS[gi][1]
+            if GROUPS[gi][0] == 0:
+                at = LOAD_AT[0] + P - 1
+                nc.vector.tensor_copy(out=g_tiles[(gi, 0)][0:1, at : at + 1], in_=corner[0:1, 0:1])
             for t in (3, 2, 1, 0):
                 words = g_tiles[(gi, t)][:].bitcast(I32).rearrange("p (g w) -> p g w", g=count)
                 d0 = LOAD_AT[t] // 2

@@ -47,7 +47,7 @@ def tile_subsampledrelativeattention_t_kernel(tc, q, e, grad_out, out):
         const = ctx.enter_context(tc.tile_pool(name="const", bufs=1))
         gpool = ctx.enter_context(tc.tile_pool(name="gpool", bufs=1))
         work = ctx.enter_context(tc.tile_pool(name="work", bufs=3))
-        opool = ctx.enter_context(tc.tile_pool(name="opool", bufs=6))
+        opool = ctx.enter_context(tc.tile_pool(name="opool", bufs=16))
         pst = ctx.enter_context(tc.psum_pool(name="pst", bufs=2))
         pso = ctx.enter_context(tc.psum_pool(name="pso", bufs=4))
         ctx.enter_context(tc.manual_schedule())
@@ -56,20 +56,6 @@ def tile_subsampledrelativeattention_t_kernel(tc, q, e, grad_out, out):
         make_identity(nc, ident[:])
         zero = const.tile([P, P], F32, name="zero")
         nc.vector.memset(zero[:], 0.0)
-        idx = const.tile([P, 64], I32, name="idx")
-        nc.gpsimd.iota(idx[:], pattern=[[2, 64]], base=0, channel_multiplier=1)
-        keep_lo = const.tile([P, 64], I32, name="keep_lo")
-        keep_hi = const.tile([P, 64], I32, name="keep_hi")
-        keep_hs = const.tile([P, 64], I32, name="keep_hs")
-        mask = const.tile([P, 64], I32, name="mask")
-        nc.vector.tensor_scalar(
-            out=keep_lo[:], in0=idx[:], scalar1=127.0, scalar2=65535.0, op0=ALU.is_ge, op1=ALU.mult
-        )
-        nc.vector.tensor_scalar(
-            out=keep_hi[:], in0=idx[:], scalar1=126.0, scalar2=65535.0, op0=ALU.is_ge, op1=ALU.mult
-        )
-        nc.vector.tensor_single_scalar(out=keep_hs[:], in_=keep_hi[:], scalar=16, op=ALU.logical_shift_left)
-        nc.vector.tensor_tensor(out=mask[:], in0=keep_lo[:], in1=keep_hs[:], op=ALU.bitwise_or)
 
         e_raw = [None, None]
         g_tiles = {}
@@ -143,15 +129,18 @@ def tile_subsampledrelativeattention_t_kernel(tc, q, e, grad_out, out):
             count = GROUPS[gi][1]
             if GROUPS[gi][0] == 0:
                 at = LOAD_AT[0] + P - 1
-                nc.vector.tensor_copy(out=g_tiles[(gi, 0)][0:1, at : at + 1], in_=corner[0:1, 0:1])
+                nc.gpsimd.tensor_copy(out=g_tiles[(gi, 0)][0:1, at : at + 1], in_=corner[0:1, 0:1])
             for t in (3, 2, 1, 0):
-                words = g_tiles[(gi, t)][:].bitcast(I32).rearrange("p (g w) -> p g w", g=count)
-                d0 = LOAD_AT[t] // 2
-                nc.vector.tensor_tensor(
-                    out=words[:, :, d0 : d0 + 64],
-                    in0=words[:, :, d0 : d0 + 64],
-                    in1=mask[:].unsqueeze(1).to_broadcast([P, count, 64]),
-                    op=ALU.bitwise_and,
+                cols = g_tiles[(gi, t)][:].rearrange("p (g w) -> p g w", g=count)
+                d0 = LOAD_AT[t]
+                nc.gpsimd.affine_select(
+                    out=cols[:, :, d0 : d0 + P],
+                    in_=cols[:, :, d0 : d0 + P],
+                    pattern=[[0, count], [1, P]],
+                    compare_op=ALU.is_ge,
+                    fill=0.0,
+                    base=1 - P,
+                    channel_multiplier=1,
                 )
 
         def transposes(n):
@@ -216,17 +205,11 @@ def tile_subsampledrelativeattention_t_kernel(tc, q, e, grad_out, out):
             if not last:
                 nc.sync.dma_start(out=rows, in_=osb[:].rearrange("p (s d) -> p s d", s=4))
 
-        first_of_group = {}
-        at_n = 0
         for gi in range(len(GROUPS)):
-            first_of_group[at_n] = gi
-            at_n += GROUPS[gi][1]
-
+            clear_left_of_diagonal(gi)
         regroup_e(1)
-        clear_left_of_diagonal(0)
         transposes(0)
         copy_out(0)
-        clear_left_of_diagonal(1)
         transposes(1)
         regroup_e(0)
         for n in range(n_mats):
@@ -235,13 +218,10 @@ def tile_subsampledrelativeattention_t_kernel(tc, q, e, grad_out, out):
                 quantise_e(1)
                 copy_out(1)
                 quantise_e(0)
-                clear_left_of_diagonal(2)
             else:
                 if n + 1 < n_mats:
                     copy_out(n + 1)
                 quantise(n)
-                if n + 3 in first_of_group:
-                    clear_left_of_diagonal(first_of_group[n + 3])
             if n + 2 < n_mats:
                 transposes(n + 2)
             multiply_and_store(n)

@@ -24,6 +24,7 @@ BYTES = NB * L * L * 4 + 2 * L * L * 2 + NB * (L * (L + 1) // 2) * 2
 TILE_COLS = (256, 256, 512, 512)
 LOAD_AT = (128, 0, 128, 0)
 GROUPS = ((15, 1), (14, 1), (12, 2), (8, 4), (4, 4), (0, 4))
+E_CUT = 84
 
 
 def tile_subsampledrelativeattention_t_kernel(tc, q, e, grad_out, out):
@@ -48,7 +49,7 @@ def tile_subsampledrelativeattention_t_kernel(tc, q, e, grad_out, out):
         gpool = ctx.enter_context(tc.tile_pool(name="gpool", bufs=1))
         work = ctx.enter_context(tc.tile_pool(name="work", bufs=3))
         opool = ctx.enter_context(tc.tile_pool(name="opool", bufs=16))
-        pst = ctx.enter_context(tc.psum_pool(name="pst", bufs=2))
+        pst = ctx.enter_context(tc.psum_pool(name="pst", bufs=1))
         pso = ctx.enter_context(tc.psum_pool(name="pso", bufs=4))
         ctx.enter_context(tc.manual_schedule())
 
@@ -110,13 +111,14 @@ def tile_subsampledrelativeattention_t_kernel(tc, q, e, grad_out, out):
         banks = {}
         grouped = {}
         codes = {}
+        left = {}
 
         def regroup_e(h):
             e_grp[h] = const.tile([P, 4 * L], BF16, name="e_grp%d" % h, align_bytes=64)
-            nc.scalar.copy(
-                out=e_grp[h][:].rearrange("p (c i t) -> p c t i", i=4, t=4),
-                in_=e_raw[h][:].rearrange("p (t c i) -> p c t i", t=4, i=4),
-            )
+            dst = e_grp[h][:].rearrange("p (c i t) -> p c t i", i=4, t=4)
+            src = e_raw[h][:].rearrange("p (t c i) -> p c t i", t=4, i=4)
+            nc.vector.tensor_copy(out=dst[:, 0:E_CUT], in_=src[:, 0:E_CUT])
+            nc.scalar.copy(out=dst[:, E_CUT:], in_=src[:, E_CUT:])
 
         def quantise_e(h):
             nc.vector.quantize_mx(
@@ -143,17 +145,25 @@ def tile_subsampledrelativeattention_t_kernel(tc, q, e, grad_out, out):
                     channel_multiplier=1,
                 )
 
+        bank_pairs = []
+        for k in range(2):
+            xa = pst.tile([P, L], F32, name="xa%d" % k)
+            xb = pst.tile([P, L], F32, name="xb%d" % k)
+            bank_pairs.append((xa, xb))
+            for t in range(2):
+                nc.tensor.transpose(xa[:, t * 256 : t * 256 + P], zero[:], ident[:])
+
         def transposes(n):
             gi, g = seq[n]
             count = GROUPS[gi][1]
-            xa = pst.tile([P, L], F32, name="xa")
-            xb = pst.tile([P, L], F32, name="xb")
-            banks[n] = (xa, xb)
+            banks[n] = bank_pairs[n % 2]
             for t in (3, 2, 1, 0):
                 fw = g_tiles[(gi, t)][:].bitcast(F32).rearrange("p (g w) -> p g w", g=count)
                 for u in range(2):
+                    if t < 2 and u == 0:
+                        continue
                     if t < 2:
-                        src = zero[:] if u == 0 else fw[:, g, 0:P]
+                        src = fw[:, g, 0:P]
                     else:
                         src = fw[:, g, u * P : (u + 1) * P]
                     at = (t % 2) * 256 + u * P
@@ -181,6 +191,7 @@ def tile_subsampledrelativeattention_t_kernel(tc, q, e, grad_out, out):
             h = bh % 2
             g_codes, g_scales = codes[n]
             last = n == n_mats - 1
+            leave = n % 2 == 1 and not last
             osb = opool.tile([P, 4 * L], F32, name="osb")
             rows = out[bh // 2, h].rearrange("(c s) d -> c s d", s=4)
             for s in range(4):
@@ -200,10 +211,17 @@ def tile_subsampledrelativeattention_t_kernel(tc, q, e, grad_out, out):
                         out=rows[:, s - 1 : s + 1, :],
                         in_=osb[:, (s - 1) * L : (s + 1) * L].rearrange("p (s d) -> p s d", s=2),
                     )
+                elif leave and s == 3:
+                    left[n] = (acc, osb, rows)
                 else:
                     nc.scalar.copy(out=osb[:, s * L : (s + 1) * L], in_=acc[:])
-            if not last:
+            if not last and not leave:
                 nc.sync.dma_start(out=rows, in_=osb[:].rearrange("p (s d) -> p s d", s=4))
+
+        def finish(n):
+            acc, osb, rows = left[n]
+            nc.vector.tensor_copy(out=osb[:, 3 * L : 4 * L], in_=acc[:])
+            nc.sync.dma_start(out=rows, in_=osb[:].rearrange("p (s d) -> p s d", s=4))
 
         for gi in range(len(GROUPS)):
             clear_left_of_diagonal(gi)
@@ -211,17 +229,19 @@ def tile_subsampledrelativeattention_t_kernel(tc, q, e, grad_out, out):
         transposes(0)
         copy_out(0)
         transposes(1)
-        regroup_e(0)
         for n in range(n_mats):
             if n == 0:
-                quantise(0)
                 quantise_e(1)
+                quantise(0)
+                regroup_e(0)
                 copy_out(1)
                 quantise_e(0)
             else:
                 if n + 1 < n_mats:
                     copy_out(n + 1)
                 quantise(n)
+                if n - 1 in left:
+                    finish(n - 1)
             if n + 2 < n_mats:
                 transposes(n + 2)
             multiply_and_store(n)

@@ -17,13 +17,15 @@ NB = 16
 L = 512
 LL = L * L
 SKEW = L + 1
+RUN = 4 * SKEW
+HALF = RUN // 4
+PAIRS = NB // 2
+ROW_W = 257
+MASK_W = 129
 
 FLOPS = 2 * NB * L * L * L
 BYTES = NB * L * L * 4 + 2 * L * L * 2 + NB * (L * (L + 1) // 2) * 2
 
-TILE_COLS = (256, 256, 512, 512)
-LOAD_AT = (128, 0, 128, 0)
-GROUPS = ((15, 1), (14, 1), (12, 2), (8, 4), (4, 4), (0, 4))
 E_CUT = 84
 
 
@@ -47,8 +49,9 @@ def tile_subsampledrelativeattention_t_kernel(tc, q, e, grad_out, out):
     with ExitStack() as ctx:
         const = ctx.enter_context(tc.tile_pool(name="const", bufs=1))
         gpool = ctx.enter_context(tc.tile_pool(name="gpool", bufs=1))
-        work = ctx.enter_context(tc.tile_pool(name="work", bufs=3))
-        opool = ctx.enter_context(tc.tile_pool(name="opool", bufs=16))
+        work = ctx.enter_context(tc.tile_pool(name="work", bufs=2))
+        cpool = ctx.enter_context(tc.tile_pool(name="cpool", bufs=3))
+        opool = ctx.enter_context(tc.tile_pool(name="opool", bufs=10))
         pst = ctx.enter_context(tc.psum_pool(name="pst", bufs=1))
         pso = ctx.enter_context(tc.psum_pool(name="pso", bufs=4))
         ctx.enter_context(tc.manual_schedule())
@@ -58,9 +61,19 @@ def tile_subsampledrelativeattention_t_kernel(tc, q, e, grad_out, out):
         zero = const.tile([P, P], F32, name="zero")
         nc.vector.memset(zero[:], 0.0)
 
-        e_raw = [None, None]
-        g_tiles = {}
+        up = {}
+        lo_raw = {}
+        lo_fix = {}
         corner = const.tile([1, 2], BF16, name="corner")
+        for k in range(PAIRS):
+            lo_raw[k] = gpool.tile([P, RUN], BF16, name="lo_raw%d" % k)
+            lo_fix[k] = gpool.tile([P, 2 * L], BF16, name="lo_fix%d" % k)
+            for t in range(2):
+                up[(k, t)] = gpool.tile([P, 2 * 256], BF16, name="up%d_%d" % (k, t))
+            nc.vector.memset(up[(k, 0)][:].bitcast(I32).rearrange("p (g w) -> p g w", g=2)[:, :, 0:64], 0)
+        nc.vector.memset(up[(PAIRS - 1, 0)][0:1, P : 2 * P], 0.0)
+
+        e_raw = [None, None]
 
         def load_e(h):
             raw = const.tile([P, 4 * L], BF16, name="e_raw%d" % h)
@@ -70,48 +83,60 @@ def tile_subsampledrelativeattention_t_kernel(tc, q, e, grad_out, out):
             )
             e_raw[h] = raw
 
-        def load_group(gi):
-            b0, count = GROUPS[gi]
-            for t in (3, 2, 1, 0):
-                gt = gpool.tile([P, count * TILE_COLS[t]], BF16, name="g%d_%d" % (gi, t))
-                words = gt[:].bitcast(I32).rearrange("p (g w) -> p g w", g=count)
-                cols = gt[:].rearrange("p (g w) -> p g w", g=count)
-                lo = LOAD_AT[t]
-                width = P * (t + 1)
-                if lo:
-                    nc.vector.memset(words[:, :, 0 : lo // 2], 0)
-                if t == 0 and b0 == 0:
-                    nc.vector.memset(gt[0:1, lo : lo + P], 0.0)
+        def load_pair(k):
+            b0 = NB - 2 - 2 * k
+            first = 2 * P * SKEW - L
+            for g in range(2):
+                nc.sync.dma_start(
+                    out=lo_raw[k][g:P:2, :],
+                    in_=mats[b0 + g, first : first + 64 * RUN].rearrange("(c x) -> c x", x=RUN),
+                )
+            nc.sync.dma_start(out=up[(k, 1)][:].rearrange("p (g w) -> p g w", g=2), in_=skewed(b0, 2, 1))
+            cols = up[(k, 0)][:].rearrange("p (g w) -> p g w", g=2)
+            if b0 == 0:
+                nc.sync.dma_start(out=cols[:, 1:2, P : 2 * P], in_=skewed(1, 1, 0))
+                for r0, r1 in ((16, P), (1, 16)):
+                    at = SKEW * r0 - P
                     nc.sync.dma_start(
-                        out=cols[:, 1:count, lo : lo + width], in_=skewed(1, count - 1, 0)
+                        out=up[(k, 0)][r0:r1, P : 2 * P],
+                        in_=flat[at : at + (r1 - r0) * SKEW].rearrange("(i c) -> i c", c=SKEW)[:, 1 : 1 + P],
                     )
-                    for r0, r1 in ((16, P), (1, 16)):
-                        first = SKEW * r0 - P
-                        nc.sync.dma_start(
-                            out=gt[r0:r1, lo : lo + P],
-                            in_=flat[first : first + (r1 - r0) * SKEW].rearrange("(i c) -> i c", c=SKEW)[:, 1 : 1 + P],
-                        )
-                    nc.sync.dma_start(out=corner[:], in_=flat[0:2].rearrange("(a b) -> a b", a=1))
-                else:
-                    nc.sync.dma_start(out=cols[:, :, lo : lo + width], in_=skewed(b0, count, t))
-                g_tiles[(gi, t)] = gt
+                nc.sync.dma_start(out=corner[:], in_=flat[0:2].rearrange("(a b) -> a b", a=1))
+            else:
+                nc.sync.dma_start(out=cols[:, :, P : 2 * P], in_=skewed(b0, 2, 0))
 
-        load_group(0)
-        load_e(1)
-        load_group(1)
+        load_pair(0)
         load_e(0)
-        for gi in range(2, len(GROUPS)):
-            load_group(gi)
+        load_e(1)
+        for k in range(1, PAIRS):
+            load_pair(k)
+
+        pidx = const.tile([P, 1], I32, name="pidx")
+        nc.gpsimd.iota(pidx[:], pattern=[[0, 1]], base=0, channel_multiplier=1)
+        idx = const.tile([P, 4 * MASK_W], I32, name="idx")
+        nc.gpsimd.iota(idx[:], pattern=[[2, 2], [2, 2], [2, MASK_W]], base=0, channel_multiplier=0)
+        chalf = const.tile([P, 1], I32, name="chalf")
+        limit_lo = const.tile([P, 1], F32, name="limit_lo")
+        limit_hi = const.tile([P, 1], F32, name="limit_hi")
+        nc.vector.tensor_single_scalar(out=chalf[:], in_=pidx[:], scalar=1, op=ALU.arith_shift_right)
+        nc.vector.tensor_scalar(out=limit_lo[:], in0=chalf[:], scalar1=-4.0, scalar2=256.0, op0=ALU.mult, op1=ALU.add)
+        nc.vector.tensor_scalar(out=limit_hi[:], in0=chalf[:], scalar1=-4.0, scalar2=255.0, op0=ALU.mult, op1=ALU.add)
+        keep_lo = const.tile([P, 4 * MASK_W], I32, name="keep_lo")
+        keep_hi = const.tile([P, 4 * MASK_W], I32, name="keep_hi")
+        lo_mask = const.tile([P, 4 * MASK_W], I32, name="lo_mask")
+        nc.vector.tensor_scalar(
+            out=keep_lo[:], in0=idx[:], scalar1=limit_lo[:, 0:1], scalar2=65535.0, op0=ALU.is_ge, op1=ALU.mult
+        )
+        nc.vector.tensor_scalar(
+            out=keep_hi[:], in0=idx[:], scalar1=limit_hi[:, 0:1], scalar2=-65536.0, op0=ALU.is_ge, op1=ALU.mult
+        )
+        nc.vector.tensor_tensor(out=lo_mask[:], in0=keep_lo[:], in1=keep_hi[:], op=ALU.bitwise_or)
 
         e_codes = const.tile([P, 2 * L], U32, name="e_codes", align_bytes=64)
         e_scales = const.tile([P, 2 * L], U8, name="e_scales", align_bytes=64)
         e_grp = {}
-        seq = [(gi, g) for gi in range(len(GROUPS)) for g in range(GROUPS[gi][1])]
-        n_mats = len(seq)
-        banks = {}
         grouped = {}
         codes = {}
-        left = {}
 
         def regroup_e(h):
             e_grp[h] = const.tile([P, 4 * L], BF16, name="e_grp%d" % h, align_bytes=64)
@@ -127,121 +152,148 @@ def tile_subsampledrelativeattention_t_kernel(tc, q, e, grad_out, out):
                 in_=e_grp[h][:],
             )
 
-        def clear_left_of_diagonal(gi):
-            count = GROUPS[gi][1]
-            if GROUPS[gi][0] == 0:
-                at = LOAD_AT[0] + P - 1
-                nc.gpsimd.tensor_copy(out=g_tiles[(gi, 0)][0:1, at : at + 1], in_=corner[0:1, 0:1])
-            for t in (3, 2, 1, 0):
-                cols = g_tiles[(gi, t)][:].rearrange("p (g w) -> p g w", g=count)
-                d0 = LOAD_AT[t]
+        def clear_left_of_diagonal(k):
+            words = lo_raw[k][:].bitcast(I32).rearrange("p (q w) -> p q w", q=2)
+            by_row = lo_mask[:].rearrange("p (q r w) -> p q r w", q=2, r=2)
+            for r in (1, 0):
+                nc.vector.tensor_tensor(
+                    out=words[:, :, r * ROW_W : r * ROW_W + MASK_W],
+                    in0=words[:, :, r * ROW_W : r * ROW_W + MASK_W],
+                    in1=by_row[:, :, r, :],
+                    op=ALU.bitwise_and,
+                )
+            if k == PAIRS - 1:
+                nc.gpsimd.tensor_copy(out=up[(k, 0)][0:1, 2 * P - 1 : 2 * P], in_=corner[0:1, 0:1])
+            for t in (1, 0):
+                cols = up[(k, t)][:].rearrange("p (g w) -> p g w", g=2)
+                d0 = P * (1 - t)
                 nc.gpsimd.affine_select(
                     out=cols[:, :, d0 : d0 + P],
                     in_=cols[:, :, d0 : d0 + P],
-                    pattern=[[0, count], [1, P]],
+                    pattern=[[0, 2], [1, P]],
                     compare_op=ALU.is_ge,
                     fill=0.0,
                     base=1 - P,
                     channel_multiplier=1,
                 )
+            nc.gpsimd.tensor_scalar(
+                out=lo_fix[k][:].rearrange("p (q m) -> p q m", q=2),
+                in0=lo_raw[k][:].rearrange("p (q x) -> p q x", q=2)[:, :, 1 : 1 + L],
+                scalar1=1.0,
+                scalar2=0.0,
+                op0=ALU.mult,
+                op1=ALU.add,
+            )
 
-        bank_pairs = []
-        for k in range(2):
-            xa = pst.tile([P, L], F32, name="xa%d" % k)
-            xb = pst.tile([P, L], F32, name="xb%d" % k)
-            bank_pairs.append((xa, xb))
+        up_bank = []
+        lo_bank = []
+        for g in range(2):
+            ub = pst.tile([P, L], F32, name="ub%d" % g)
+            lb = pst.tile([P, L], F32, name="lb%d" % g)
+            up_bank.append(ub)
+            lo_bank.append(lb)
             for t in range(2):
-                nc.tensor.transpose(xa[:, t * 256 : t * 256 + P], zero[:], ident[:])
+                nc.tensor.transpose(ub[:, t * 256 : t * 256 + P], zero[:], ident[:])
 
-        def transposes(n):
-            gi, g = seq[n]
-            count = GROUPS[gi][1]
-            banks[n] = bank_pairs[n % 2]
-            for t in (3, 2, 1, 0):
-                fw = g_tiles[(gi, t)][:].bitcast(F32).rearrange("p (g w) -> p g w", g=count)
+        def transposes_up(k):
+            for g in range(2):
+                for t in range(2):
+                    fw = up[(k, t)][:].bitcast(F32).rearrange("p (g w) -> p g w", g=2)
+                    nc.tensor.transpose(up_bank[g][:, t * 256 + P : t * 256 + 2 * P], fw[:, g, :], ident[:])
+
+        def transposes_lo(k):
+            fixw = lo_fix[k][:].bitcast(F32)
+            raww = lo_raw[k][:].bitcast(F32)
+            for qq in range(2):
                 for u in range(2):
-                    if t < 2 and u == 0:
-                        continue
-                    if t < 2:
-                        src = fw[:, g, 0:P]
-                    else:
-                        src = fw[:, g, u * P : (u + 1) * P]
-                    at = (t % 2) * 256 + u * P
-                    nc.tensor.transpose(banks[n][t // 2][:, at : at + P], src, ident[:])
-
-        def copy_out(n):
-            grp = work.tile([P, 4 * L], BF16, name="grp", align_bytes=64)
-            grouped[n] = grp
-            gw = grp[:].bitcast(F32).rearrange("p (s b c u) -> p s b c u", s=4, b=4, c=32, u=2)
-            for half in (1, 0):
-                nc.vector.tensor_copy(
-                    out=gw[:, :, 2 * half : 2 * half + 2, :, :],
-                    in_=banks[n][half][:].rearrange("p (b u c s) -> p s b c u", b=2, u=2, c=32, s=4),
-                )
-
-        def quantise(n):
-            g_codes = work.tile([P, L], U32, name="g_codes", align_bytes=64)
-            g_scales = work.tile([P, L], U8, name="g_scales", align_bytes=64)
-            codes[n] = (g_codes, g_scales)
-            nc.vector.quantize_mx(out=g_codes[:].bitcast(E5X4), scales=g_scales[:], in_=grouped[n][:])
-
-        def multiply_and_store(n):
-            gi, g = seq[n]
-            bh = GROUPS[gi][0] + g
-            h = bh % 2
-            g_codes, g_scales = codes[n]
-            last = n == n_mats - 1
-            leave = n % 2 == 1 and not last
-            osb = opool.tile([P, 4 * L], F32, name="osb")
-            rows = out[bh // 2, h].rearrange("(c s) d -> c s d", s=4)
-            for s in range(4):
-                acc = pso.tile([P, L], F32, name="acc")
-                nc.tensor.matmul_mx(
-                    out=acc[:],
-                    lhsT=g_codes[:, s * P : (s + 1) * P].bitcast(E5X4),
-                    lhsT_scale=g_scales[:, s * P : (s + 1) * P],
-                    rhs=e_codes[:, h * L : (h + 1) * L].bitcast(E4X4),
-                    rhs_scale=e_scales[:, h * L : (h + 1) * L],
-                    start=True,
-                    stop=True,
-                )
-                if last and s % 2 == 1:
-                    nc.vector.tensor_copy(out=osb[:, s * L : (s + 1) * L], in_=acc[:])
-                    nc.sync.dma_start(
-                        out=rows[:, s - 1 : s + 1, :],
-                        in_=osb[:, (s - 1) * L : (s + 1) * L].rearrange("p (s d) -> p s d", s=2),
+                    at = qq * HALF + ROW_W + u * P
+                    nc.tensor.transpose(lo_bank[qq][:, 256 + u * P : 256 + (u + 1) * P], raww[:, at : at + P], ident[:])
+            for qq in range(2):
+                for u in range(2):
+                    nc.tensor.transpose(
+                        lo_bank[qq][:, u * P : (u + 1) * P], fixw[:, qq * 256 + u * P : qq * 256 + (u + 1) * P], ident[:]
                     )
-                elif leave and s == 3:
-                    left[n] = (acc, osb, rows)
+
+        def copy_out_up(k):
+            grp = work.tile([P, 8 * L], BF16, name="grp", align_bytes=64)
+            grouped[k] = grp
+            gw_up = grp[:].bitcast(F32).rearrange("p (g s b c u) -> p g s b c u", g=2, s=4, b=4, c=32, u=2)
+            for g in range(2):
+                src = up_bank[g][:].rearrange("p (b u c s) -> p s b c u", b=2, u=2, c=32, s=4)
+                if k < 2:
+                    nc.scalar.copy(out=gw_up[:, g, :, 0:2, :, :], in_=src)
                 else:
-                    nc.scalar.copy(out=osb[:, s * L : (s + 1) * L], in_=acc[:])
-            if not last and not leave:
-                nc.sync.dma_start(out=rows, in_=osb[:].rearrange("p (s d) -> p s d", s=4))
+                    nc.vector.tensor_copy(out=gw_up[:, g, :, 0:2, :, :], in_=src)
 
-        def finish(n):
-            acc, osb, rows = left[n]
-            nc.vector.tensor_copy(out=osb[:, 3 * L : 4 * L], in_=acc[:])
-            nc.sync.dma_start(out=rows, in_=osb[:].rearrange("p (s d) -> p s d", s=4))
+        def copy_out_lo(k):
+            gw_lo = grouped[k][:].bitcast(F32).rearrange("p (g s c u) -> p g s c u", g=2, s=4, c=P, u=2)
+            for qq in range(2):
+                nc.vector.tensor_copy(
+                    out=gw_lo[:, :, 2 * qq : 2 * qq + 2, 64:P, :],
+                    in_=lo_bank[qq][:].rearrange("p (s u c g) -> p g s c u", s=2, u=2, c=64, g=2),
+                )
 
-        for gi in range(len(GROUPS)):
-            clear_left_of_diagonal(gi)
-        regroup_e(1)
-        transposes(0)
-        copy_out(0)
-        transposes(1)
-        for n in range(n_mats):
-            if n == 0:
-                quantise_e(1)
-                quantise(0)
+        def quantise(k):
+            g_codes = cpool.tile([P, 2 * L], U32, name="g_codes", align_bytes=64)
+            g_scales = cpool.tile([P, 2 * L], U8, name="g_scales", align_bytes=64)
+            codes[k] = (g_codes, g_scales)
+            nc.vector.quantize_mx(out=g_codes[:].bitcast(E5X4), scales=g_scales[:], in_=grouped[k][:])
+
+        def multiply_and_store(k, h):
+            g_codes, g_scales = codes[k]
+            last = k == PAIRS - 1
+            if True:
+                osb = opool.tile([P, 4 * L], F32, name="osb")
+                rows = out[PAIRS - 1 - k, h].rearrange("(c s) d -> c s d", s=4)
+                for s in range(4):
+                    acc = pso.tile([P, L], F32, name="acc")
+                    at = h * L + s * P
+                    nc.tensor.matmul_mx(
+                        out=acc[:],
+                        lhsT=g_codes[:, at : at + P].bitcast(E5X4),
+                        lhsT_scale=g_scales[:, at : at + P],
+                        rhs=e_codes[:, h * L : (h + 1) * L].bitcast(E4X4),
+                        rhs_scale=e_scales[:, h * L : (h + 1) * L],
+                        start=True,
+                        stop=True,
+                    )
+                    by_vector = last and s % 2 == 1
+                    if by_vector:
+                        nc.vector.tensor_copy(out=osb[:, s * L : (s + 1) * L], in_=acc[:])
+                    else:
+                        nc.scalar.copy(out=osb[:, s * L : (s + 1) * L], in_=acc[:])
+                    if last and s % 2 == 1:
+                        nc.sync.dma_start(
+                            out=rows[:, s - 1 : s + 1, :],
+                            in_=osb[:, (s - 1) * L : (s + 1) * L].rearrange("p (s d) -> p s d", s=2),
+                        )
+                if not last:
+                    nc.sync.dma_start(out=rows, in_=osb[:].rearrange("p (s d) -> p s d", s=4))
+
+        for k in range(3):
+            clear_left_of_diagonal(k)
+            if k == 0:
                 regroup_e(0)
-                copy_out(1)
-                quantise_e(0)
-            else:
-                if n + 1 < n_mats:
-                    copy_out(n + 1)
-                quantise(n)
-                if n - 1 in left:
-                    finish(n - 1)
-            if n + 2 < n_mats:
-                transposes(n + 2)
-            multiply_and_store(n)
+                regroup_e(1)
+        transposes_lo(0)
+        transposes_up(0)
+        copy_out_up(0)
+        copy_out_lo(0)
+        quantise_e(0)
+        quantise(0)
+        quantise_e(1)
+        transposes_up(1)
+        copy_out_up(1)
+        for k in range(PAIRS):
+            if k + 1 < PAIRS:
+                transposes_lo(k + 1)
+                copy_out_lo(k + 1)
+            if k + 3 < PAIRS:
+                clear_left_of_diagonal(k + 3)
+            multiply_and_store(k, 0)
+            if k + 1 < PAIRS:
+                quantise(k + 1)
+            if k + 2 < PAIRS:
+                transposes_up(k + 2)
+                copy_out_up(k + 2)
+            multiply_and_store(k, 1)

from contextlib import ExitStack

import concourse.mybir as mybir
from concourse.masks import make_identity

BF16 = mybir.dt.bfloat16
F32 = mybir.dt.float32
I32 = mybir.dt.int32
U32 = mybir.dt.uint32
U8 = mybir.dt.uint8
E4X4 = mybir.dt.float8_e4m3fn_x4
E5X4 = mybir.dt.float8_e5m2_x4
ALU = mybir.AluOpType

P = 128
NB = 16
L = 512
LL = L * L
SKEW = L + 1
RUN = 4 * SKEW
HALF = RUN // 4
PAIRS = NB // 2
ROW_W = 257
MASK_W = 129

FLOPS = 2 * NB * L * L * L
BYTES = NB * L * L * 4 + 2 * L * L * 2 + NB * (L * (L + 1) // 2) * 2

E_CUT = 84


def tile_subsampledrelativeattention_t_kernel(tc, q, e, grad_out, out):
    nc = tc.nc
    flat = grad_out.rearrange("b h i j -> (b h i j)")
    mats = grad_out.rearrange("b h i j -> (b h) (i j)")

    def skewed(b0, count, t):
        width = P * (t + 1)
        if t == 0:
            start = b0 * LL - P
            src = flat[start : start + count * LL].rearrange("(g x) -> g x", x=LL)
            first = 0
        else:
            src = mats[b0 : b0 + count, :]
            first = 65536 * t - P
        rows = src[:, first : first + P * SKEW].rearrange("g (i c) -> i g c", c=SKEW)
        return rows[:, :, 1 : 1 + width]

    with ExitStack() as ctx:
        const = ctx.enter_context(tc.tile_pool(name="const", bufs=1))
        gpool = ctx.enter_context(tc.tile_pool(name="gpool", bufs=1))
        work = ctx.enter_context(tc.tile_pool(name="work", bufs=2))
        cpool = ctx.enter_context(tc.tile_pool(name="cpool", bufs=3))
        opool = ctx.enter_context(tc.tile_pool(name="opool", bufs=10))
        pst = ctx.enter_context(tc.psum_pool(name="pst", bufs=1))
        pso = ctx.enter_context(tc.psum_pool(name="pso", bufs=4))
        ctx.enter_context(tc.manual_schedule())

        ident = const.tile([P, P], F32, name="ident")
        make_identity(nc, ident[:])
        zero = const.tile([P, P], F32, name="zero")
        nc.vector.memset(zero[:], 0.0)

        up = {}
        lo_raw = {}
        lo_fix = {}
        corner = const.tile([1, 2], BF16, name="corner")
        for k in range(PAIRS):
            lo_raw[k] = gpool.tile([P, RUN], BF16, name="lo_raw%d" % k)
            lo_fix[k] = gpool.tile([P, 2 * L], BF16, name="lo_fix%d" % k)
            for t in range(2):
                up[(k, t)] = gpool.tile([P, 2 * 256], BF16, name="up%d_%d" % (k, t))
            nc.vector.memset(up[(k, 0)][:].bitcast(I32).rearrange("p (g w) -> p g w", g=2)[:, :, 0:64], 0)
        nc.vector.memset(up[(PAIRS - 1, 0)][0:1, P : 2 * P], 0.0)

        e_raw = [None, None]

        def load_e(h):
            raw = const.tile([P, 4 * L], BF16, name="e_raw%d" % h)
            nc.sync.dma_start(
                out=raw[:].rearrange("p (u x) -> p u x", u=2),
                in_=e[h].rearrange("(u p k) d -> p u (k d)", u=2, p=P, k=2),
            )
            e_raw[h] = raw

        def load_pair(k):
            b0 = NB - 2 - 2 * k
            first = 2 * P * SKEW - L
            for g in range(2):
                nc.sync.dma_start(
                    out=lo_raw[k][g:P:2, :],
                    in_=mats[b0 + g, first : first + 64 * RUN].rearrange("(c x) -> c x", x=RUN),
                )
            nc.sync.dma_start(out=up[(k, 1)][:].rearrange("p (g w) -> p g w", g=2), in_=skewed(b0, 2, 1))
            cols = up[(k, 0)][:].rearrange("p (g w) -> p g w", g=2)
            if b0 == 0:
                nc.sync.dma_start(out=cols[:, 1:2, P : 2 * P], in_=skewed(1, 1, 0))
                for r0, r1 in ((16, P), (1, 16)):
                    at = SKEW * r0 - P
                    nc.sync.dma_start(
                        out=up[(k, 0)][r0:r1, P : 2 * P],
                        in_=flat[at : at + (r1 - r0) * SKEW].rearrange("(i c) -> i c", c=SKEW)[:, 1 : 1 + P],
                    )
                nc.sync.dma_start(out=corner[:], in_=flat[0:2].rearrange("(a b) -> a b", a=1))
            else:
                nc.sync.dma_start(out=cols[:, :, P : 2 * P], in_=skewed(b0, 2, 0))

        load_pair(0)
        load_e(0)
        load_e(1)
        for k in range(1, PAIRS):
            load_pair(k)

        pidx = const.tile([P, 1], I32, name="pidx")
        nc.gpsimd.iota(pidx[:], pattern=[[0, 1]], base=0, channel_multiplier=1)
        idx = const.tile([P, 4 * MASK_W], I32, name="idx")
        nc.gpsimd.iota(idx[:], pattern=[[2, 2], [2, 2], [2, MASK_W]], base=0, channel_multiplier=0)
        chalf = const.tile([P, 1], I32, name="chalf")
        limit_lo = const.tile([P, 1], F32, name="limit_lo")
        limit_hi = const.tile([P, 1], F32, name="limit_hi")
        nc.vector.tensor_single_scalar(out=chalf[:], in_=pidx[:], scalar=1, op=ALU.arith_shift_right)
        nc.vector.tensor_scalar(out=limit_lo[:], in0=chalf[:], scalar1=-4.0, scalar2=256.0, op0=ALU.mult, op1=ALU.add)
        nc.vector.tensor_scalar(out=limit_hi[:], in0=chalf[:], scalar1=-4.0, scalar2=255.0, op0=ALU.mult, op1=ALU.add)
        keep_lo = const.tile([P, 4 * MASK_W], I32, name="keep_lo")
        keep_hi = const.tile([P, 4 * MASK_W], I32, name="keep_hi")
        lo_mask = const.tile([P, 4 * MASK_W], I32, name="lo_mask")
        nc.vector.tensor_scalar(
            out=keep_lo[:], in0=idx[:], scalar1=limit_lo[:, 0:1], scalar2=65535.0, op0=ALU.is_ge, op1=ALU.mult
        )
        nc.vector.tensor_scalar(
            out=keep_hi[:], in0=idx[:], scalar1=limit_hi[:, 0:1], scalar2=-65536.0, op0=ALU.is_ge, op1=ALU.mult
        )
        nc.vector.tensor_tensor(out=lo_mask[:], in0=keep_lo[:], in1=keep_hi[:], op=ALU.bitwise_or)

        e_codes = const.tile([P, 2 * L], U32, name="e_codes", align_bytes=64)
        e_scales = const.tile([P, 2 * L], U8, name="e_scales", align_bytes=64)
        e_grp = {}
        grouped = {}
        codes = {}

        def regroup_e(h):
            e_grp[h] = const.tile([P, 4 * L], BF16, name="e_grp%d" % h, align_bytes=64)
            dst = e_grp[h][:].rearrange("p (c i t) -> p c t i", i=4, t=4)
            src = e_raw[h][:].rearrange("p (t c i) -> p c t i", t=4, i=4)
            nc.vector.tensor_copy(out=dst[:, 0:E_CUT], in_=src[:, 0:E_CUT])
            nc.scalar.copy(out=dst[:, E_CUT:], in_=src[:, E_CUT:])

        def quantise_e(h):
            nc.vector.quantize_mx(
                out=e_codes[:, h * L : (h + 1) * L].bitcast(E4X4),
                scales=e_scales[:, h * L : (h + 1) * L],
                in_=e_grp[h][:],
            )

        def clear_left_of_diagonal(k):
            words = lo_raw[k][:].bitcast(I32).rearrange("p (q w) -> p q w", q=2)
            by_row = lo_mask[:].rearrange("p (q r w) -> p q r w", q=2, r=2)
            for r in (1, 0):
                nc.vector.tensor_tensor(
                    out=words[:, :, r * ROW_W : r * ROW_W + MASK_W],
                    in0=words[:, :, r * ROW_W : r * ROW_W + MASK_W],
                    in1=by_row[:, :, r, :],
                    op=ALU.bitwise_and,
                )
            if k == PAIRS - 1:
                nc.gpsimd.tensor_copy(out=up[(k, 0)][0:1, 2 * P - 1 : 2 * P], in_=corner[0:1, 0:1])
            for t in (1, 0):
                cols = up[(k, t)][:].rearrange("p (g w) -> p g w", g=2)
                d0 = P * (1 - t)
                nc.gpsimd.affine_select(
                    out=cols[:, :, d0 : d0 + P],
                    in_=cols[:, :, d0 : d0 + P],
                    pattern=[[0, 2], [1, P]],
                    compare_op=ALU.is_ge,
                    fill=0.0,
                    base=1 - P,
                    channel_multiplier=1,
                )
            nc.gpsimd.tensor_scalar(
                out=lo_fix[k][:].rearrange("p (q m) -> p q m", q=2),
                in0=lo_raw[k][:].rearrange("p (q x) -> p q x", q=2)[:, :, 1 : 1 + L],
                scalar1=1.0,
                scalar2=0.0,
                op0=ALU.mult,
                op1=ALU.add,
            )

        up_bank = []
        lo_bank = []
        for g in range(2):
            ub = pst.tile([P, L], F32, name="ub%d" % g)
            lb = pst.tile([P, L], F32, name="lb%d" % g)
            up_bank.append(ub)
            lo_bank.append(lb)
            for t in range(2):
                nc.tensor.transpose(ub[:, t * 256 : t * 256 + P], zero[:], ident[:])

        def transposes_up(k):
            for g in range(2):
                for t in range(2):
                    fw = up[(k, t)][:].bitcast(F32).rearrange("p (g w) -> p g w", g=2)
                    nc.tensor.transpose(up_bank[g][:, t * 256 + P : t * 256 + 2 * P], fw[:, g, :], ident[:])

        def transposes_lo(k):
            fixw = lo_fix[k][:].bitcast(F32)
            raww = lo_raw[k][:].bitcast(F32)
            for qq in range(2):
                for u in range(2):
                    at = qq * HALF + ROW_W + u * P
                    nc.tensor.transpose(lo_bank[qq][:, 256 + u * P : 256 + (u + 1) * P], raww[:, at : at + P], ident[:])
            for qq in range(2):
                for u in range(2):
                    nc.tensor.transpose(
                        lo_bank[qq][:, u * P : (u + 1) * P], fixw[:, qq * 256 + u * P : qq * 256 + (u + 1) * P], ident[:]
                    )

        def copy_out_up(k):
            grp = work.tile([P, 8 * L], BF16, name="grp", align_bytes=64)
            grouped[k] = grp
            gw_up = grp[:].bitcast(F32).rearrange("p (g s b c u) -> p g s b c u", g=2, s=4, b=4, c=32, u=2)
            for g in range(2):
                src = up_bank[g][:].rearrange("p (b u c s) -> p s b c u", b=2, u=2, c=32, s=4)
                if k < 2:
                    nc.scalar.copy(out=gw_up[:, g, :, 0:2, :, :], in_=src)
                else:
                    nc.vector.tensor_copy(out=gw_up[:, g, :, 0:2, :, :], in_=src)

        def copy_out_lo(k):
            gw_lo = grouped[k][:].bitcast(F32).rearrange("p (g s c u) -> p g s c u", g=2, s=4, c=P, u=2)
            for qq in range(2):
                nc.vector.tensor_copy(
                    out=gw_lo[:, :, 2 * qq : 2 * qq + 2, 64:P, :],
                    in_=lo_bank[qq][:].rearrange("p (s u c g) -> p g s c u", s=2, u=2, c=64, g=2),
                )

        def quantise(k):
            g_codes = cpool.tile([P, 2 * L], U32, name="g_codes", align_bytes=64)
            g_scales = cpool.tile([P, 2 * L], U8, name="g_scales", align_bytes=64)
            codes[k] = (g_codes, g_scales)
            nc.vector.quantize_mx(out=g_codes[:].bitcast(E5X4), scales=g_scales[:], in_=grouped[k][:])

        def multiply_and_store(k, h):
            g_codes, g_scales = codes[k]
            last = k == PAIRS - 1
            if True:
                osb = opool.tile([P, 4 * L], F32, name="osb")
                rows = out[PAIRS - 1 - k, h].rearrange("(c s) d -> c s d", s=4)
                for s in range(4):
                    acc = pso.tile([P, L], F32, name="acc")
                    at = h * L + s * P
                    nc.tensor.matmul_mx(
                        out=acc[:],
                        lhsT=g_codes[:, at : at + P].bitcast(E5X4),
                        lhsT_scale=g_scales[:, at : at + P],
                        rhs=e_codes[:, h * L : (h + 1) * L].bitcast(E4X4),
                        rhs_scale=e_scales[:, h * L : (h + 1) * L],
                        start=True,
                        stop=True,
                    )
                    by_vector = last and s % 2 == 1
                    if by_vector:
                        nc.vector.tensor_copy(out=osb[:, s * L : (s + 1) * L], in_=acc[:])
                    else:
                        nc.scalar.copy(out=osb[:, s * L : (s + 1) * L], in_=acc[:])
                    if last and s % 2 == 1:
                        nc.sync.dma_start(
                            out=rows[:, s - 1 : s + 1, :],
                            in_=osb[:, (s - 1) * L : (s + 1) * L].rearrange("p (s d) -> p s d", s=2),
                        )
                if not last:
                    nc.sync.dma_start(out=rows, in_=osb[:].rearrange("p (s d) -> p s d", s=4))

        for k in range(3):
            clear_left_of_diagonal(k)
            if k == 0:
                regroup_e(0)
                regroup_e(1)
        transposes_lo(0)
        transposes_up(0)
        copy_out_up(0)
        copy_out_lo(0)
        quantise_e(0)
        quantise(0)
        quantise_e(1)
        transposes_up(1)
        copy_out_up(1)
        for k in range(PAIRS):
            if k + 1 < PAIRS:
                transposes_lo(k + 1)
                copy_out_lo(k + 1)
            if k + 3 < PAIRS:
                clear_left_of_diagonal(k + 3)
            multiply_and_store(k, 0)
            if k + 1 < PAIRS:
                quantise(k + 1)
            if k + 2 < PAIRS:
                transposes_up(k + 2)
                copy_out_up(k + 2)
            multiply_and_store(k, 1)
